import numpy as np
import ml_dtypes


BF16 = ml_dtypes.bfloat16


def bf(x):
    return np.asarray(x, np.float32).astype(BF16)


def f64(x):
    return np.asarray(x).astype(np.float64)


E2M1 = np.array([0.0, 0.5, 1.0, 1.5, 2.0, 3.0, 4.0, 6.0, -0.0, -0.5, -1.0, -1.5, -2.0, -3.0, -4.0, -6.0])


def pack_weight(w, fmt):
    k, n = w.shape
    w = f64(bf(w)).reshape(k // 32, 32, n)
    amax = np.abs(w).max(1)
    if fmt == "e4m3":
        byte = np.frexp(amax)[1] - 1 + 127 - 7
    else:
        mant, ex = np.frexp(amax / 6.0)
        byte = np.where(mant > 0.5, ex, ex - 1) + 127
    byte = np.clip(np.where(amax > 0, byte, 1), 1, 254)
    scaled = (w * np.exp2(127.0 - byte)[:, None, :]).reshape(k, n).astype(np.float32)
    by_word = np.ascontiguousarray(scaled.reshape(k // 512, 128, 4, n).transpose(0, 1, 3, 2))
    if fmt == "e4m3":
        words = by_word.astype(ml_dtypes.float8_e4m3fn).view(np.uint8)
    else:
        c = by_word.astype(ml_dtypes.float4_e2m1fn).view(np.uint8) & 0xF
        words = c[..., 0::2] | (c[..., 1::2] << 4)
    return np.ascontiguousarray(words), np.ascontiguousarray(byte.astype(np.uint8).reshape(k // 512, 16, n))


def unpack_weight(words, scales, fmt):
    g, p, n, _ = words.shape
    if fmt == "e4m3":
        vals = np.ascontiguousarray(words).view(ml_dtypes.float8_e4m3fn).astype(np.float64)
    else:
        nib = np.empty((g, p, n, 4), np.uint8)
        nib[..., 0::2] = words & 0xF
        nib[..., 1::2] = words >> 4
        vals = E2M1[nib]
    vals = vals * np.repeat(np.exp2(scales.astype(np.float64) - 127.0), 8, axis=1)[..., None]
    return vals.transpose(0, 1, 3, 2).reshape(g * 512, n)

def pack4(w):
    words, scales = pack_weight(w, "e2m1")
    return words.reshape(words.shape[0], 128, -1), scales


def unpack4(words, scales):
    return unpack_weight(words.reshape(words.shape[0], 128, -1, 2), scales, "e2m1")


def kspread(k):
    return np.exp2(np.repeat(np.random.randint(-6, 7, k // 32), 32).astype(np.float64))


B, T, C, F = 4, 1024, 1024, 4096
M = T


def silu(v):
    return v / (1.0 + np.exp(-v))


def sigmoid(v):
    return 1.0 / (1.0 + np.exp(-v))


def setup_inputs():
    t = kspread(F)
    x = np.random.standard_normal((B, T, C)) + 0.5 * np.random.standard_normal((B, 1, C))
    h = silu(np.random.standard_normal((B, T, F)) * 0.85) * t
    h_words, h_scales = pack4(h.reshape(B * T, F).T)
    memory = bf(np.random.standard_normal((1, M, C)) * 6.0 / np.sqrt(C))
    w2_words, w2_scales = pack4(np.random.standard_normal((F, C)) * 3.0 / np.sqrt(F) / t[:, None])
    b2 = bf(np.random.standard_normal(C) * 0.5)
    return {"h_words": h_words,
            "h_scales": h_scales,
            "x": bf(x),
            "memory": memory,
            "w2_words": w2_words,
            "w2_scales": w2_scales,
            "b2": b2}


def reference(h_words, h_scales, x, memory, w2_words, w2_scales, b2):
    h = unpack4(h_words, h_scales).T.reshape(B, T, F)
    update_gate = sigmoid((h @ unpack4(w2_words, w2_scales)) + f64(b2))
    x_mean = f64(x).mean(axis=1, keepdims=True)
    new_mem = f64(memory) * (1.0 - update_gate) + x_mean * update_gate
    return new_mem.mean(axis=0, keepdims=True)

@@ -1,0 +1,308 @@
+from contextlib import ExitStack
+
+import concourse.mybir as mybir
+from concourse.masks import make_identity
+
+FLOPS = 2 * 4096 * 4096 * 1024
+
+F32 = mybir.dt.float32
+BF16 = mybir.dt.bfloat16
+U8 = mybir.dt.uint8
+I32 = mybir.dt.int32
+FP4X4 = mybir.dt.float4_e2m1fn_x4
+ALU = mybir.AluOpType
+ACT = mybir.ActivationFunctionType
+AX = mybir.AxisListType
+
+P = 128
+NB = 4
+G = 8
+NCT = 8
+NMH = 2
+SWEEP = 6
+HEAD_RUNS = ((0, 1), (1, 4), (4, 8))
+X_ON_PE = (0, 1)
+OUT_GROUPS = (((0, 8),), ((0, 4), (4, 2), (6, 1), (7, 1)))
+
+
+def tile_dynamicmemorybank_pb_kernel(tc, h_words, h_scales, x, memory, w2_words, w2_scales, b2, out):
+    nc = tc.nc
+    with ExitStack() as ctx:
+        keep = ctx.enter_context(tc.tile_pool(name="keep", bufs=1))
+        big = ctx.enter_context(tc.tile_pool(name="big", bufs=3))
+        hpool = ctx.enter_context(tc.tile_pool(name="hcodes", bufs=2))
+        r8 = ctx.enter_context(tc.tile_pool(name="r8", bufs=2))
+        gpool = ctx.enter_context(tc.tile_pool(name="gate", bufs=8))
+        tmp = ctx.enter_context(tc.tile_pool(name="tmp", bufs=2))
+        accp = ctx.enter_context(tc.psum_pool(name="acc", bufs=SWEEP))
+        auxp = ctx.enter_context(tc.psum_pool(name="aux", bufs=1))
+
+        w2c = keep.tile([P, G, 2048], U8, name="w2c", align_bytes=64)
+        w2s = keep.tile([P, G, 1024], U8, name="w2s", align_bytes=64)
+        hs = [
+            keep.tile([P, G, 1024], U8, name="hs0", align_bytes=64),
+            keep.tile([P, G, 1024], U8, name="hs1", align_bytes=64),
+        ]
+        mem_t = keep.tile([P, 8192], BF16, name="mem_t", align_bytes=64)
+        base = keep.tile([P, 8192], F32, name="base", align_bytes=64)
+        ident = keep.tile([P, P], F32, name="ident")
+        i4 = keep.tile([P, 32], F32, name="i4")
+        mfull = keep.tile([P, P], F32, name="mfull")
+        ones = keep.tile([P, 32], BF16, name="ones")
+        b2row = keep.tile([P, 1, 1024], BF16, name="b2row")
+        b2col = keep.tile([P, NCT], F32, name="b2col")
+        xm = keep.tile([P, NB, NCT], F32, name="xm")
+        ysum = keep.tile([P, NB + 1, 32], F32, name="ysum")
+        warm = keep.tile([P, 1], F32, name="warm")
+
+        def load_codes(dst, words, g0, g1, lo, hi):
+            nc.sync.dma_start(
+                out=dst[:, g0:g1, :].bitcast(I32),
+                in_=words[g0:g1, :, lo:hi].rearrange("g p n -> p g n").bitcast(I32),
+            )
+
+        def load_scales(dst, scales, g0, g1, lo, hi):
+            for q in range(4):
+                nc.sync.dma_start(
+                    out=dst[32 * q : 32 * q + 4, g0:g1, :].bitcast(I32),
+                    in_=scales[g0:g1, 4 * q : 4 * q + 4, lo:hi].rearrange("g r n -> r g n").bitcast(I32),
+                )
+
+        def load_x(b):
+            xt = big.tile([P, 8, 1024], BF16, name="xt", tag="big", align_bytes=64)
+            nc.sync.dma_start(out=xt[:], in_=x[b].rearrange("(p j) c -> p j c", j=8))
+            return xt
+
+        def load_h(b):
+            hc = hpool.tile([P, G, 2048], U8, name="hc", align_bytes=64)
+            load_codes(hc, h_words, 0, G, 2048 * b, 2048 * (b + 1))
+            load_scales(hs[b % 2], h_scales, 0, G, 1024 * b, 1024 * (b + 1))
+            return hc
+
+        nc.gpsimd.memset(warm[:], 0.0)
+        nc.scalar.activation(out=warm[:], in_=warm[:], func=ACT.Sigmoid)
+        nc.gpsimd.memset(b2row[:], 0.0)
+        nc.scalar.dma_start(out=b2row[0:1, 0, :], in_=b2.rearrange("(o c) -> o c", o=1))
+        nc.gpsimd.memset(ones[:], 1.0)
+        make_identity(nc, ident[:])
+
+        w2raw = big.tile([P, G, 2048], U8, name="w2raw", tag="big", align_bytes=64)
+        w2sraw = r8.tile([P, G, 1024], U8, name="w2sraw", tag="r8", align_bytes=64)
+        hcs = {}
+        hcs[0] = hpool.tile([P, G, 2048], U8, name="hc", align_bytes=64)
+        for g0, g1 in HEAD_RUNS:
+            nc.vector.memset(w2sraw[:, g0:g1, :].bitcast(I32), 0)
+            nc.vector.memset(hs[0][:, g0:g1, :].bitcast(I32), 0)
+        nc.vector.memset(hs[1][:].bitcast(I32), 0)
+        nc.vector.memset(ysum[:], 0.0)
+        for g0, g1 in HEAD_RUNS:
+            load_codes(w2raw, w2_words, g0, g1, 0, 2048)
+            load_codes(hcs[0], h_words, g0, g1, 0, 2048)
+            load_scales(w2sraw, w2_scales, g0, g1, 0, 1024)
+            load_scales(hs[0], h_scales, g0, g1, 0, 1024)
+            for g in range(g0, g1):
+                nc.vector.tensor_copy(
+                    out=w2c[:, g, :].bitcast(I32).rearrange("p (ct a w) -> p ct a w", ct=8, a=4),
+                    in_=w2raw[:, g, :].bitcast(I32).rearrange("p (a ct w) -> p ct a w", a=4, ct=8),
+                )
+                nc.vector.tensor_copy(
+                    out=w2s[:, g, :].bitcast(I32).rearrange("p (ct a w) -> p ct a w", ct=8, a=4),
+                    in_=w2sraw[:, g, :].bitcast(I32).rearrange("p (a ct w) -> p ct a w", a=4, ct=8),
+                )
+        nc.vector.tensor_reduce(out=i4[:], in_=ident[:].rearrange("p (q j) -> p j q", q=4), axis=AX.X, op=ALU.add)
+        for a in range(4):
+            nc.vector.tensor_copy(out=mfull[:, 32 * a : 32 * a + 32], in_=i4[:])
+
+        xts = {}
+        xts[0] = load_x(0)
+        lraw = big.tile([P, 32, 256], BF16, name="lraw", tag="big", align_bytes=64)
+        for mh in range(NMH):
+            for a in range(4):
+                nc.sync.dma_start(
+                    out=lraw[32 * a : 32 * a + 32, 16 * mh : 16 * mh + 16, :],
+                    in_=memory[0, 512 * mh : 512 * mh + 512, 256 * a : 256 * a + 256].rearrange(
+                        "(mb i) c -> i mb c", i=32
+                    ),
+                )
+        hcs[1] = load_h(1)
+        xts[1] = load_x(1)
+
+        def sums_on_tensor(src, nj, slot):
+            psx = auxp.tile([P, 8, 32], F32, name="psx")
+            for t in range(8):
+                for j in range(nj):
+                    nc.tensor.matmul(
+                        out=psx[:, t, :],
+                        lhsT=src[:, j, 128 * t : 128 * t + 128],
+                        rhs=ones[:],
+                        start=(j == 0),
+                        stop=(j == nj - 1),
+                    )
+            for s in range(4):
+                nc.scalar.copy(out=ysum[32 * s : 32 * s + 32, slot, s:32:4], in_=psx[32 * s : 32 * s + 32, :, 0])
+
+        def spread(slot, dst, scale):
+            ps2 = auxp.tile([P, 32], F32, name="ps2")
+            nc.tensor.matmul(out=ps2[:], lhsT=mfull[:], rhs=ysum[:, slot, :], start=True, stop=True)
+            for a in range(4):
+                nc.scalar.activation(
+                    out=dst[32 * a : 32 * a + 32, :],
+                    in_=ps2[32 * a : 32 * a + 32, 8 * a : 8 * a + 8],
+                    func=ACT.Copy,
+                    scale=scale,
+                )
+
+        def tree_pieces(b):
+            xt = xts[b]
+            st = {}
+
+            def l1(hf):
+                cs = slice(512 * hf, 512 * hf + 512)
+                st[hf] = tmp.tile([P, 4, 512], F32, name="s1")
+                nc.vector.tensor_tensor(out=st[hf][:], in0=xt[:, 0:4, cs], in1=xt[:, 4:8, cs], op=ALU.add)
+
+            def l2(hf):
+                nc.vector.tensor_tensor(out=st[hf][:, 0:2, :], in0=st[hf][:, 0:2, :], in1=st[hf][:, 2:4, :], op=ALU.add)
+
+            def l3(hf):
+                if hf == 0:
+                    st["z"] = tmp.tile([P, 1024], F32, name="zsum", bufs=1, align_bytes=64)
+                nc.vector.tensor_tensor(
+                    out=st["z"][:, 512 * hf : 512 * hf + 512], in0=st[hf][:, 0, :], in1=st[hf][:, 1, :], op=ALU.add
+                )
+
+            def tr():
+                st["zt"] = tmp.tile([P, 1024], F32, name="zt", bufs=1, align_bytes=64)
+                nc.vector.transpose(out=st["zt"][:], in_=st["z"][:])
+
+            def red():
+                nc.vector.tensor_reduce(
+                    out=ysum[:, b + 1, :], in_=st["zt"][:].rearrange("p (cb j) -> p cb j", j=32), axis=AX.X, op=ALU.add
+                )
+                spread(b + 1, xm[:, b, :], 1.0 / 1024.0)
+
+            return [
+                lambda: l1(0),
+                lambda: l1(1),
+                lambda: l2(0),
+                lambda: l2(1),
+                lambda: l3(0),
+                lambda: l3(1),
+                tr,
+                red,
+            ]
+
+        def mx_pass(acc, b, mh, ct, g):
+            nc.tensor.matmul_mx(
+                out=acc[:],
+                lhsT=w2c[:, g, 256 * ct : 256 * ct + 256].bitcast(FP4X4),
+                lhsT_scale=w2s[:, g, 128 * ct : 128 * ct + 128],
+                rhs=hcs[b][:, g, 1024 * mh : 1024 * mh + 1024].bitcast(FP4X4),
+                rhs_scale=hs[b % 2][:, g, 512 * mh : 512 * mh + 512],
+                start=(g == 0),
+                stop=(g == G - 1),
+            )
+
+        def mem_view(mh, ct):
+            return mem_t[:].rearrange("p (mb ct i) -> p mb ct i", ct=8, i=32)[:, 16 * mh : 16 * mh + 16, ct, :]
+
+        def region(mh, ct):
+            off = 4096 * mh
+            for c0, n in OUT_GROUPS[mh]:
+                if c0 <= ct < c0 + n:
+                    return off, c0, n
+                off += 512 * n
+            raise ValueError("no region")
+
+        def base_view(mh, ct):
+            off, c0, n = region(mh, ct)
+            return base[:, off : off + 512 * n].rearrange("p (mb c i) -> p mb c i", c=n, i=32)[:, :, ct - c0, :]
+
+        def weigh(gt, b, mh, ct):
+            gv = gt[:].rearrange("p (mb i) -> p mb i", i=32)
+            nc.vector.scalar_tensor_tensor(
+                out=gv, in0=mem_view(mh, ct), scalar=xm[:, b, ct : ct + 1], in1=gv, op0=ALU.subtract, op1=ALU.mult
+            )
+
+        def emit(mh, ct):
+            off, c0, n = region(mh, ct)
+            total = 512 * n
+            step = min(total, 2048)
+            for e0 in range(0, total, step):
+                rt = r8.tile([P, 2048], F32, name="rt", tag="r8", align_bytes=64)
+                nc.vector.transpose(out=rt[:, 0:step], in_=base[:, off + e0 : off + e0 + step])
+                nmb = step // (32 * n)
+                rows = 512 * mh + 32 * (e0 // (32 * n))
+                for a in range(4):
+                    nc.sync.dma_start(
+                        out=out[0, rows : rows + 32 * nmb, 256 * a + 32 * c0 : 256 * a + 32 * (c0 + n)].rearrange(
+                            "(mb i) c -> i mb c", i=32
+                        ),
+                        in_=rt[32 * a : 32 * a + 32, 0:step].rearrange("p (mb c) -> p mb c", c=32 * n),
+                    )
+
+        def blend(gt, b, mh, ct):
+            gv = gt[:].rearrange("p (mb i) -> p mb i", i=32)
+            prev = mem_view(mh, ct) if b == 0 else base_view(mh, ct)
+            nc.vector.scalar_tensor_tensor(
+                out=base_view(mh, ct), in0=gv, scalar=-0.25, in1=prev, op0=ALU.mult, op1=ALU.add
+            )
+            if b == NB - 1:
+                c0, n = region(mh, ct)[1:]
+                if ct == c0 + n - 1:
+                    emit(mh, ct)
+
+        sums_on_tensor(b2row, 1, 0)
+        spread(0, b2col[:], 1.0)
+
+        order = [(b, mh, ct) for b in range(NB) for mh in range(NMH) for ct in range(NCT)]
+        accs = {}
+        for k in range(SWEEP):
+            accs[k] = accp.tile([P, 512], F32, name="acc")
+        for g in range(G):
+            for k in range(SWEEP):
+                mx_pass(accs[k], order[k][0], order[k][1], order[k][2], g)
+
+        sums_on_tensor(xts[0], 8, 1)
+        spread(1, xm[:, 0, :], 1.0 / 1024.0)
+        xts[2] = load_x(2)
+        lflat = lraw[:].rearrange("p mb c -> p (mb c)")
+        for k in range(4):
+            nc.vector.transpose(out=mem_t[:, 2048 * k : 2048 * k + 2048], in_=lflat[:, 2048 * k : 2048 * k + 2048])
+        xts[3] = load_x(3)
+
+        def mean_on_tensor(b):
+            def run():
+                sums_on_tensor(xts[b], 8, b + 1)
+                spread(b + 1, xm[:, b, :], 1.0 / 1024.0)
+
+            return run
+
+        filler = []
+        first = 2
+        pending = []
+        for k in range(len(order)):
+            b, mh, ct = order[k]
+            idx = k % (NMH * NCT)
+            if idx == 0 and b + 1 < NB:
+                filler = tree_pieces(b + 1)
+                first = 2
+                if b + 1 in X_ON_PE:
+                    filler = [mean_on_tensor(b + 1)]
+                    first = 10
+            if k >= SWEEP:
+                accs[k] = accp.tile([P, 512], F32, name="acc")
+                for g in range(G):
+                    mx_pass(accs[k], b, mh, ct, g)
+            gt = gpool.tile([P, 512], F32, name="gt")
+            nc.scalar.activation(out=gt[:], in_=accs[k][:], func=ACT.Sigmoid, bias=b2col[:, ct : ct + 1], scale=1.0)
+            weigh(gt, b, mh, ct)
+            if pending:
+                blend(pending[0], pending[1], pending[2], pending[3])
+            pending = [gt, b, mh, ct]
+            if idx >= first and filler:
+                filler[0]()
+                filler = filler[1:]
+            if idx == NMH * NCT - 1 and b + 2 < NB:
+                hcs[b + 2] = load_h(b + 2)
+        blend(pending[0], pending[1], pending[2], pending[3])

@@ -19,30 +19,31 @@ NB = 4
 G = 8
 NCT = 8
 NMH = 2
-SWEEP = 6
+SWEEP = 7
 HEAD_RUNS = ((0, 1), (1, 4), (4, 8))
-X_ON_PE = (0, 1)
-OUT_GROUPS = (((0, 8),), ((0, 4), (4, 2), (6, 1), (7, 1)))
+OUT_GROUPS = (((0, 2), (2, 2), (4, 2), (6, 2)), ((0, 2), (2, 2), (4, 2), (6, 1), (7, 1)))
+SUMS_AT = {2: 26, 3: 29}
+SPREAD_AT = {0: 12, 1: 18, 2: 27, 3: 30}
+TREES = (0, 1)
+VECTOR_SLOTS = (1, 2)
 
 
 def tile_dynamicmemorybank_pb_kernel(tc, h_words, h_scales, x, memory, w2_words, w2_scales, b2, out):
     nc = tc.nc
     with ExitStack() as ctx:
+        ctx.enter_context(tc.manual_schedule(engines={mybir.EngineType.PE, mybir.EngineType.Activation}))
         keep = ctx.enter_context(tc.tile_pool(name="keep", bufs=1))
         big = ctx.enter_context(tc.tile_pool(name="big", bufs=3))
-        hpool = ctx.enter_context(tc.tile_pool(name="hcodes", bufs=2))
-        r8 = ctx.enter_context(tc.tile_pool(name="r8", bufs=2))
-        gpool = ctx.enter_context(tc.tile_pool(name="gate", bufs=8))
+        hpool = ctx.enter_context(tc.tile_pool(name="hcodes", bufs=4))
+        fpool = ctx.enter_context(tc.tile_pool(name="final", bufs=2))
+        gpool = ctx.enter_context(tc.tile_pool(name="gate", bufs=11))
         tmp = ctx.enter_context(tc.tile_pool(name="tmp", bufs=2))
         accp = ctx.enter_context(tc.psum_pool(name="acc", bufs=SWEEP))
         auxp = ctx.enter_context(tc.psum_pool(name="aux", bufs=1))
 
         w2c = keep.tile([P, G, 2048], U8, name="w2c", align_bytes=64)
         w2s = keep.tile([P, G, 1024], U8, name="w2s", align_bytes=64)
-        hs = [
-            keep.tile([P, G, 1024], U8, name="hs0", align_bytes=64),
-            keep.tile([P, G, 1024], U8, name="hs1", align_bytes=64),
-        ]
+        hs = [keep.tile([P, G, 512], U8, name="hs%d" % i, align_bytes=64) for i in range(4)]
         mem_t = keep.tile([P, 8192], BF16, name="mem_t", align_bytes=64)
         base = keep.tile([P, 8192], F32, name="base", align_bytes=64)
         ident = keep.tile([P, P], F32, name="ident")
@@ -54,6 +55,8 @@ def tile_dynamicmemorybank_pb_kernel(tc, h_words, h_scales, x, memory, w2_words,
         xm = keep.tile([P, NB, NCT], F32, name="xm")
         ysum = keep.tile([P, NB + 1, 32], F32, name="ysum")
         warm = keep.tile([P, 1], F32, name="warm")
+        mem_v = mem_t[:].rearrange("p (mb ct i) -> p mb ct i", ct=NCT, i=32)
+        base_v = base[:].rearrange("p (mb ct i) -> p mb ct i", ct=NCT, i=32)
 
         def load_codes(dst, words, g0, g1, lo, hi):
             nc.sync.dma_start(
@@ -73,11 +76,14 @@ def tile_dynamicmemorybank_pb_kernel(tc, h_words, h_scales, x, memory, w2_words,
             nc.sync.dma_start(out=xt[:], in_=x[b].rearrange("(p j) c -> p j c", j=8))
             return xt
 
-        def load_h(b):
-            hc = hpool.tile([P, G, 2048], U8, name="hc", align_bytes=64)
-            load_codes(hc, h_words, 0, G, 2048 * b, 2048 * (b + 1))
-            load_scales(hs[b % 2], h_scales, 0, G, 1024 * b, 1024 * (b + 1))
-            return hc
+        hcs = {}
+        state = {"pending": None, "fin": None, "next": 0, "aux": None}
+
+        def load_h(b, mh):
+            tok = 1024 * b + 512 * mh
+            hcs[(b, mh)] = hpool.tile([P, G, 1024], U8, name="hc", align_bytes=64)
+            load_codes(hcs[(b, mh)], h_words, 0, G, 2 * tok, 2 * tok + 1024)
+            load_scales(hs[(2 * b + mh) % 4], h_scales, 0, G, tok, tok + 512)
 
         nc.gpsimd.memset(warm[:], 0.0)
         nc.scalar.activation(out=warm[:], in_=warm[:], func=ACT.Sigmoid)
@@ -87,19 +93,19 @@ def tile_dynamicmemorybank_pb_kernel(tc, h_words, h_scales, x, memory, w2_words,
         make_identity(nc, ident[:])
 
         w2raw = big.tile([P, G, 2048], U8, name="w2raw", tag="big", align_bytes=64)
-        w2sraw = r8.tile([P, G, 1024], U8, name="w2sraw", tag="r8", align_bytes=64)
-        hcs = {}
-        hcs[0] = hpool.tile([P, G, 2048], U8, name="hc", align_bytes=64)
+        w2sraw = tmp.tile([P, G, 1024], U8, name="w2sraw", tag="s1", align_bytes=64)
+        hcs[(0, 0)] = hpool.tile([P, G, 1024], U8, name="hc", align_bytes=64)
         for g0, g1 in HEAD_RUNS:
             nc.vector.memset(w2sraw[:, g0:g1, :].bitcast(I32), 0)
             nc.vector.memset(hs[0][:, g0:g1, :].bitcast(I32), 0)
-        nc.vector.memset(hs[1][:].bitcast(I32), 0)
+        for i in range(1, 4):
+            nc.vector.memset(hs[i][:].bitcast(I32), 0)
         nc.vector.memset(ysum[:], 0.0)
         for g0, g1 in HEAD_RUNS:
             load_codes(w2raw, w2_words, g0, g1, 0, 2048)
-            load_codes(hcs[0], h_words, g0, g1, 0, 2048)
+            load_codes(hcs[(0, 0)], h_words, g0, g1, 0, 1024)
             load_scales(w2sraw, w2_scales, g0, g1, 0, 1024)
-            load_scales(hs[0], h_scales, g0, g1, 0, 1024)
+            load_scales(hs[0], h_scales, g0, g1, 0, 512)
             for g in range(g0, g1):
                 nc.vector.tensor_copy(
                     out=w2c[:, g, :].bitcast(I32).rearrange("p (ct a w) -> p ct a w", ct=8, a=4),
@@ -112,9 +118,12 @@ def tile_dynamicmemorybank_pb_kernel(tc, h_words, h_scales, x, memory, w2_words,
         nc.vector.tensor_reduce(out=i4[:], in_=ident[:].rearrange("p (q j) -> p j q", q=4), axis=AX.X, op=ALU.add)
         for a in range(4):
             nc.vector.tensor_copy(out=mfull[:, 32 * a : 32 * a + 32], in_=i4[:])
-
+        load_h(0, 1)
         xts = {}
         xts[0] = load_x(0)
+        xts[1] = load_x(1)
+        load_h(1, 0)
+        load_h(1, 1)
         lraw = big.tile([P, 32, 256], BF16, name="lraw", tag="big", align_bytes=64)
         for mh in range(NMH):
             for a in range(4):
@@ -124,11 +133,11 @@ def tile_dynamicmemorybank_pb_kernel(tc, h_words, h_scales, x, memory, w2_words,
                         "(mb i) c -> i mb c", i=32
                     ),
                 )
-        hcs[1] = load_h(1)
-        xts[1] = load_x(1)
 
         def sums_on_tensor(src, nj, slot):
-            psx = auxp.tile([P, 8, 32], F32, name="psx")
+            aux = auxp.tile([P, 9, 32], F32, name="aux")
+            state["aux"] = aux
+            psx = aux[:, 0:8, :]
             for t in range(8):
                 for j in range(nj):
                     nc.tensor.matmul(
@@ -142,8 +151,10 @@ def tile_dynamicmemorybank_pb_kernel(tc, h_words, h_scales, x, memory, w2_words,
                 nc.scalar.copy(out=ysum[32 * s : 32 * s + 32, slot, s:32:4], in_=psx[32 * s : 32 * s + 32, :, 0])
 
         def spread(slot, dst, scale):
-            ps2 = auxp.tile([P, 32], F32, name="ps2")
-            nc.tensor.matmul(out=ps2[:], lhsT=mfull[:], rhs=ysum[:, slot, :], start=True, stop=True)
+            if slot in VECTOR_SLOTS:
+                state["aux"] = auxp.tile([P, 9, 32], F32, name="aux")
+            ps2 = state["aux"][:, 8, :]
+            nc.tensor.matmul(out=ps2, lhsT=mfull[:], rhs=ysum[:, slot, :], start=True, stop=True)
             for a in range(4):
                 nc.scalar.activation(
                     out=dst[32 * a : 32 * a + 32, :],
@@ -152,157 +163,135 @@ def tile_dynamicmemorybank_pb_kernel(tc, h_words, h_scales, x, memory, w2_words,
                     scale=scale,
                 )
 
-        def tree_pieces(b):
+        def sums_on_vector(b):
             xt = xts[b]
-            st = {}
-
-            def l1(hf):
+            s1 = []
+            for hf in range(2):
+                s1.append(tmp.tile([P, 4, 512], F32, name="s1", tag="s1", align_bytes=64))
+            zsum = tmp.tile([P, 1024], F32, name="zsum", bufs=1, align_bytes=64)
+            zt = tmp.tile([P, 1024], F32, name="zt", bufs=1, align_bytes=64)
+            for hf in range(2):
                 cs = slice(512 * hf, 512 * hf + 512)
-                st[hf] = tmp.tile([P, 4, 512], F32, name="s1")
-                nc.vector.tensor_tensor(out=st[hf][:], in0=xt[:, 0:4, cs], in1=xt[:, 4:8, cs], op=ALU.add)
-
-            def l2(hf):
-                nc.vector.tensor_tensor(out=st[hf][:, 0:2, :], in0=st[hf][:, 0:2, :], in1=st[hf][:, 2:4, :], op=ALU.add)
-
-            def l3(hf):
-                if hf == 0:
-                    st["z"] = tmp.tile([P, 1024], F32, name="zsum", bufs=1, align_bytes=64)
+                nc.vector.tensor_tensor(out=s1[hf][:], in0=xt[:, 0:4, cs], in1=xt[:, 4:8, cs], op=ALU.add)
+            for hf in range(2):
+                nc.vector.tensor_tensor(out=s1[hf][:, 0:2, :], in0=s1[hf][:, 0:2, :], in1=s1[hf][:, 2:4, :], op=ALU.add)
+            for hf in range(2):
                 nc.vector.tensor_tensor(
-                    out=st["z"][:, 512 * hf : 512 * hf + 512], in0=st[hf][:, 0, :], in1=st[hf][:, 1, :], op=ALU.add
+                    out=zsum[:, 512 * hf : 512 * hf + 512], in0=s1[hf][:, 0, :], in1=s1[hf][:, 1, :], op=ALU.add
                 )
-
-            def tr():
-                st["zt"] = tmp.tile([P, 1024], F32, name="zt", bufs=1, align_bytes=64)
-                nc.vector.transpose(out=st["zt"][:], in_=st["z"][:])
-
-            def red():
-                nc.vector.tensor_reduce(
-                    out=ysum[:, b + 1, :], in_=st["zt"][:].rearrange("p (cb j) -> p cb j", j=32), axis=AX.X, op=ALU.add
-                )
-                spread(b + 1, xm[:, b, :], 1.0 / 1024.0)
-
-            return [
-                lambda: l1(0),
-                lambda: l1(1),
-                lambda: l2(0),
-                lambda: l2(1),
-                lambda: l3(0),
-                lambda: l3(1),
-                tr,
-                red,
-            ]
+            nc.vector.transpose(out=zt[:], in_=zsum[:])
+            nc.vector.tensor_reduce(
+                out=ysum[:, b + 1, :], in_=zt[:].rearrange("p (cb j) -> p cb j", j=32), axis=AX.X, op=ALU.add
+            )
 
         def mx_pass(acc, b, mh, ct, g):
             nc.tensor.matmul_mx(
                 out=acc[:],
                 lhsT=w2c[:, g, 256 * ct : 256 * ct + 256].bitcast(FP4X4),
                 lhsT_scale=w2s[:, g, 128 * ct : 128 * ct + 128],
-                rhs=hcs[b][:, g, 1024 * mh : 1024 * mh + 1024].bitcast(FP4X4),
-                rhs_scale=hs[b % 2][:, g, 512 * mh : 512 * mh + 512],
+                rhs=hcs[(b, mh)][:, g, :].bitcast(FP4X4),
+                rhs_scale=hs[(2 * b + mh) % 4][:, g, :],
                 start=(g == 0),
                 stop=(g == G - 1),
             )
 
-        def mem_view(mh, ct):
-            return mem_t[:].rearrange("p (mb ct i) -> p mb ct i", ct=8, i=32)[:, 16 * mh : 16 * mh + 16, ct, :]
+        def emit(fin, mh, c0, n):
+            size = 512 * n
+            rt = fpool.tile([P, 1024], F32, name="rt", align_bytes=64)
+            nc.vector.transpose(out=rt[:, 0:size], in_=fin[:, 0:size])
+            for a in range(4):
+                nc.sync.dma_start(
+                    out=out[0, 512 * mh : 512 * mh + 512, 256 * a + 32 * c0 : 256 * a + 32 * (c0 + n)].rearrange(
+                        "(mb i) c -> i mb c", i=32
+                    ),
+                    in_=rt[32 * a : 32 * a + 32, 0:size].rearrange("p (mb c) -> p mb c", c=32 * n),
+                )
 
-        def region(mh, ct):
-            off = 4096 * mh
-            for c0, n in OUT_GROUPS[mh]:
-                if c0 <= ct < c0 + n:
-                    return off, c0, n
-                off += 512 * n
-            raise ValueError("no region")
+        waiting = []
+        published = []
 
-        def base_view(mh, ct):
-            off, c0, n = region(mh, ct)
-            return base[:, off : off + 512 * n].rearrange("p (mb c i) -> p mb c i", c=n, i=32)[:, :, ct - c0, :]
-
-        def weigh(gt, b, mh, ct):
-            gv = gt[:].rearrange("p (mb i) -> p mb i", i=32)
+        def blend(job):
             nc.vector.scalar_tensor_tensor(
-                out=gv, in0=mem_view(mh, ct), scalar=xm[:, b, ct : ct + 1], in1=gv, op0=ALU.subtract, op1=ALU.mult
+                out=job["dst"], in0=job["gv"], scalar=-0.25, in1=job["prev"], op0=ALU.mult, op1=ALU.add
             )
+            if job["done"]:
+                emit(job["done"][0], job["done"][1], job["done"][2], job["done"][3])
 
-        def emit(mh, ct):
-            off, c0, n = region(mh, ct)
-            total = 512 * n
-            step = min(total, 2048)
-            for e0 in range(0, total, step):
-                rt = r8.tile([P, 2048], F32, name="rt", tag="r8", align_bytes=64)
-                nc.vector.transpose(out=rt[:, 0:step], in_=base[:, off + e0 : off + e0 + step])
-                nmb = step // (32 * n)
-                rows = 512 * mh + 32 * (e0 // (32 * n))
-                for a in range(4):
-                    nc.sync.dma_start(
-                        out=out[0, rows : rows + 32 * nmb, 256 * a + 32 * c0 : 256 * a + 32 * (c0 + n)].rearrange(
-                            "(mb i) c -> i mb c", i=32
-                        ),
-                        in_=rt[32 * a : 32 * a + 32, 0:step].rearrange("p (mb c) -> p mb c", c=32 * n),
-                    )
+        def run_jobs():
+            while state["next"] < len(waiting) and waiting[state["next"]]["b"] in published:
+                job = waiting[state["next"]]
+                state["next"] += 1
+                b, mh, ct = job["b"], job["mh"], job["ct"]
+                if b == NB - 1:
+                    c0, n = [grp for grp in OUT_GROUPS[mh] if grp[0] <= ct < grp[0] + grp[1]][0]
+                    if ct == c0:
+                        state["fin"] = fpool.tile([P, 1024], F32, name="fin", align_bytes=64)
+                    fin = state["fin"]
+                    job["dst"] = fin[:, 0 : 512 * n].rearrange("p (mb c i) -> p mb c i", c=n, i=32)[:, :, ct - c0, :]
+                    if ct == c0 + n - 1:
+                        job["done"] = [fin, mh, c0, n]
+                nc.vector.scalar_tensor_tensor(
+                    out=job["gv"], in0=job["mv"], scalar=xm[:, b, ct : ct + 1], in1=job["gv"],
+                    op0=ALU.subtract, op1=ALU.mult,
+                )
+                if state["pending"]:
+                    blend(state["pending"])
+                state["pending"] = job
 
-        def blend(gt, b, mh, ct):
-            gv = gt[:].rearrange("p (mb i) -> p mb i", i=32)
-            prev = mem_view(mh, ct) if b == 0 else base_view(mh, ct)
-            nc.vector.scalar_tensor_tensor(
-                out=base_view(mh, ct), in0=gv, scalar=-0.25, in1=prev, op0=ALU.mult, op1=ALU.add
-            )
-            if b == NB - 1:
-                c0, n = region(mh, ct)[1:]
-                if ct == c0 + n - 1:
-                    emit(mh, ct)
+        order = [(b, mh, ct) for b in range(2) for mh in range(NMH) for ct in range(NCT)]
+        order.extend([(b, mh, ct) for mh in range(NMH) for ct in range(NCT) for b in (2, 3)])
+        last_use = {}
+        for k in range(len(order)):
+            last_use[(order[k][0], order[k][1])] = k
 
-        sums_on_tensor(b2row, 1, 0)
-        spread(0, b2col[:], 1.0)
-
-        order = [(b, mh, ct) for b in range(NB) for mh in range(NMH) for ct in range(NCT)]
         accs = {}
         for k in range(SWEEP):
             accs[k] = accp.tile([P, 512], F32, name="acc")
         for g in range(G):
             for k in range(SWEEP):
                 mx_pass(accs[k], order[k][0], order[k][1], order[k][2], g)
+            if g == 1:
+                sums_on_tensor(b2row, 1, 0)
+            if g == 3:
+                spread(0, b2col[:], 1.0)
 
-        sums_on_tensor(xts[0], 8, 1)
-        spread(1, xm[:, 0, :], 1.0 / 1024.0)
-        xts[2] = load_x(2)
+        for b in TREES:
+            sums_on_vector(b)
+            xts[b + 2] = load_x(b + 2)
         lflat = lraw[:].rearrange("p mb c -> p (mb c)")
-        for k in range(4):
-            nc.vector.transpose(out=mem_t[:, 2048 * k : 2048 * k + 2048], in_=lflat[:, 2048 * k : 2048 * k + 2048])
-        xts[3] = load_x(3)
+        for q in range(4):
+            nc.vector.transpose(out=mem_t[:, 2048 * q : 2048 * q + 2048], in_=lflat[:, 2048 * q : 2048 * q + 2048])
 
-        def mean_on_tensor(b):
-            def run():
-                sums_on_tensor(xts[b], 8, b + 1)
-                spread(b + 1, xm[:, b, :], 1.0 / 1024.0)
-
-            return run
-
-        filler = []
-        first = 2
-        pending = []
         for k in range(len(order)):
             b, mh, ct = order[k]
-            idx = k % (NMH * NCT)
-            if idx == 0 and b + 1 < NB:
-                filler = tree_pieces(b + 1)
-                first = 2
-                if b + 1 in X_ON_PE:
-                    filler = [mean_on_tensor(b + 1)]
-                    first = 10
+            rows = slice(16 * mh, 16 * mh + 16)
             if k >= SWEEP:
                 accs[k] = accp.tile([P, 512], F32, name="acc")
                 for g in range(G):
                     mx_pass(accs[k], b, mh, ct, g)
-            gt = gpool.tile([P, 512], F32, name="gt")
-            nc.scalar.activation(out=gt[:], in_=accs[k][:], func=ACT.Sigmoid, bias=b2col[:, ct : ct + 1], scale=1.0)
-            weigh(gt, b, mh, ct)
-            if pending:
-                blend(pending[0], pending[1], pending[2], pending[3])
-            pending = [gt, b, mh, ct]
-            if idx >= first and filler:
-                filler[0]()
-                filler = filler[1:]
-            if idx == NMH * NCT - 1 and b + 2 < NB:
-                hcs[b + 2] = load_h(b + 2)
-        blend(pending[0], pending[1], pending[2], pending[3])
+            if b == 0:
+                gv = base_v[:, rows, ct, :]
+            else:
+                gt = gpool.tile([P, 512], F32, name="gt")
+                gv = gt[:].rearrange("p (mb i) -> p mb i", i=32)
+            nc.scalar.activation(
+                out=gv,
+                in_=accs[k][:].rearrange("p (mb i) -> p mb i", i=32),
+                func=ACT.Sigmoid,
+                bias=b2col[:, ct : ct + 1],
+                scale=1.0,
+            )
+            for bb in range(NB):
+                if SUMS_AT.get(bb) == k:
+                    sums_on_tensor(xts[bb], 8, bb + 1)
+                if SPREAD_AT[bb] == k:
+                    spread(bb + 1, xm[:, bb, :], 1.0 / 1024.0)
+                    published.append(bb)
+            waiting.append(
+                {"b": b, "mh": mh, "ct": ct, "gv": gv, "mv": mem_v[:, rows, ct, :], "dst": base_v[:, rows, ct, :],
+                 "prev": mem_v[:, rows, ct, :] if b == 0 else base_v[:, rows, ct, :], "done": None}
+            )
+            run_jobs()
+            if last_use[(b, mh)] == k and b + 2 < NB:
+                load_h(b + 2, mh)
+        blend(state["pending"])

@@ -22,16 +22,17 @@ NMH = 2
 SWEEP = 7
 HEAD_RUNS = ((0, 1), (1, 4), (4, 8))
 OUT_GROUPS = (((0, 2), (2, 2), (4, 2), (6, 2)), ((0, 2), (2, 2), (4, 2), (6, 1), (7, 1)))
-SUMS_AT = {2: 26, 3: 29}
-SPREAD_AT = {0: 12, 1: 18, 2: 27, 3: 30}
+SUMS_AT = {3: 29}
+SPREAD_AT = {0: 12, 1: 18, 2: 40, 3: 30}
+LATE_TREES = {31: 2}
 TREES = (0, 1)
-VECTOR_SLOTS = (1, 2)
+VECTOR_SLOTS = (1, 2, 3)
 
 
 def tile_dynamicmemorybank_pb_kernel(tc, h_words, h_scales, x, memory, w2_words, w2_scales, b2, out):
     nc = tc.nc
     with ExitStack() as ctx:
-        ctx.enter_context(tc.manual_schedule(engines={mybir.EngineType.PE, mybir.EngineType.Activation}))
+        ctx.enter_context(tc.manual_schedule(engines={mybir.EngineType.PE, mybir.EngineType.Activation, mybir.EngineType.DVE}))
         keep = ctx.enter_context(tc.tile_pool(name="keep", bufs=1))
         big = ctx.enter_context(tc.tile_pool(name="big", bufs=3))
         hpool = ctx.enter_context(tc.tile_pool(name="hcodes", bufs=4))
@@ -88,7 +89,6 @@ def tile_dynamicmemorybank_pb_kernel(tc, h_words, h_scales, x, memory, w2_words,
         nc.gpsimd.memset(warm[:], 0.0)
         nc.scalar.activation(out=warm[:], in_=warm[:], func=ACT.Sigmoid)
         nc.gpsimd.memset(b2row[:], 0.0)
-        nc.scalar.dma_start(out=b2row[0:1, 0, :], in_=b2.rearrange("(o c) -> o c", o=1))
         nc.gpsimd.memset(ones[:], 1.0)
         make_identity(nc, ident[:])
 
@@ -98,14 +98,15 @@ def tile_dynamicmemorybank_pb_kernel(tc, h_words, h_scales, x, memory, w2_words,
         for g0, g1 in HEAD_RUNS:
             nc.vector.memset(w2sraw[:, g0:g1, :].bitcast(I32), 0)
             nc.vector.memset(hs[0][:, g0:g1, :].bitcast(I32), 0)
-        for i in range(1, 4):
-            nc.vector.memset(hs[i][:].bitcast(I32), 0)
-        nc.vector.memset(ysum[:], 0.0)
-        for g0, g1 in HEAD_RUNS:
+        later = [[ysum[:], hs[1][:].bitcast(I32)], [hs[2][:].bitcast(I32), hs[3][:].bitcast(I32)], []]
+        for run in range(len(HEAD_RUNS)):
+            g0, g1 = HEAD_RUNS[run]
             load_codes(w2raw, w2_words, g0, g1, 0, 2048)
             load_codes(hcs[(0, 0)], h_words, g0, g1, 0, 1024)
             load_scales(w2sraw, w2_scales, g0, g1, 0, 1024)
             load_scales(hs[0], h_scales, g0, g1, 0, 512)
+            if run == 0:
+                nc.sync.dma_start(out=b2row[0:1, 0, :], in_=b2.rearrange("(o c) -> o c", o=1))
             for g in range(g0, g1):
                 nc.vector.tensor_copy(
                     out=w2c[:, g, :].bitcast(I32).rearrange("p (ct a w) -> p ct a w", ct=8, a=4),
@@ -115,9 +116,14 @@ def tile_dynamicmemorybank_pb_kernel(tc, h_words, h_scales, x, memory, w2_words,
                     out=w2s[:, g, :].bitcast(I32).rearrange("p (ct a w) -> p ct a w", ct=8, a=4),
                     in_=w2sraw[:, g, :].bitcast(I32).rearrange("p (a ct w) -> p ct a w", a=4, ct=8),
                 )
-        nc.vector.tensor_reduce(out=i4[:], in_=ident[:].rearrange("p (q j) -> p j q", q=4), axis=AX.X, op=ALU.add)
-        for a in range(4):
-            nc.vector.tensor_copy(out=mfull[:, 32 * a : 32 * a + 32], in_=i4[:])
+            for view in later[run]:
+                nc.vector.memset(view, 0)
+            if run == 0:
+                nc.vector.tensor_reduce(
+                    out=i4[:], in_=ident[:].rearrange("p (q j) -> p j q", q=4), axis=AX.X, op=ALU.add
+                )
+                for a in range(4):
+                    nc.vector.tensor_copy(out=mfull[:, 32 * a : 32 * a + 32], in_=i4[:])
         load_h(0, 1)
         xts = {}
         xts[0] = load_x(0)
@@ -222,6 +228,8 @@ def tile_dynamicmemorybank_pb_kernel(tc, h_words, h_scales, x, memory, w2_words,
                 job = waiting[state["next"]]
                 state["next"] += 1
                 b, mh, ct = job["b"], job["mh"], job["ct"]
+                if (b, mh, ct) == (0, 1, 0):
+                    turn_memory(1)
                 if b == NB - 1:
                     c0, n = [grp for grp in OUT_GROUPS[mh] if grp[0] <= ct < grp[0] + grp[1]][0]
                     if ct == c0:
@@ -230,6 +238,9 @@ def tile_dynamicmemorybank_pb_kernel(tc, h_words, h_scales, x, memory, w2_words,
                     job["dst"] = fin[:, 0 : 512 * n].rearrange("p (mb c i) -> p mb c i", c=n, i=32)[:, :, ct - c0, :]
                     if ct == c0 + n - 1:
                         job["done"] = [fin, mh, c0, n]
+                if (b, mh, ct) == (NB - 1, NMH - 1, NCT - 1):
+                    blend(state["pending"])
+                    state["pending"] = None
                 nc.vector.scalar_tensor_tensor(
                     out=job["gv"], in0=job["mv"], scalar=xm[:, b, ct : ct + 1], in1=job["gv"],
                     op0=ALU.subtract, op1=ALU.mult,
@@ -259,8 +270,14 @@ def tile_dynamicmemorybank_pb_kernel(tc, h_words, h_scales, x, memory, w2_words,
             sums_on_vector(b)
             xts[b + 2] = load_x(b + 2)
         lflat = lraw[:].rearrange("p mb c -> p (mb c)")
-        for q in range(4):
-            nc.vector.transpose(out=mem_t[:, 2048 * q : 2048 * q + 2048], in_=lflat[:, 2048 * q : 2048 * q + 2048])
+
+        def turn_memory(mh):
+            for q in (2 * mh, 2 * mh + 1):
+                nc.vector.transpose(
+                    out=mem_t[:, 2048 * q : 2048 * q + 2048], in_=lflat[:, 2048 * q : 2048 * q + 2048]
+                )
+
+        turn_memory(0)
 
         for k in range(len(order)):
             b, mh, ct = order[k]
@@ -292,6 +309,8 @@ def tile_dynamicmemorybank_pb_kernel(tc, h_words, h_scales, x, memory, w2_words,
                  "prev": mem_v[:, rows, ct, :] if b == 0 else base_v[:, rows, ct, :], "done": None}
             )
             run_jobs()
+            if k in LATE_TREES:
+                sums_on_vector(LATE_TREES[k])
             if last_use[(b, mh)] == k and b + 2 < NB:
                 load_h(b + 2, mh)
         blend(state["pending"])

@@ -27,6 +27,7 @@ SPREAD_AT = {0: 12, 1: 18, 2: 40, 3: 30}
 LATE_TREES = {31: 2}
 TREES = (0, 1)
 VECTOR_SLOTS = (1, 2, 3)
+WARM_MATMULS = 16
 
 
 def tile_dynamicmemorybank_pb_kernel(tc, h_words, h_scales, x, memory, w2_words, w2_scales, b2, out):
@@ -56,6 +57,7 @@ def tile_dynamicmemorybank_pb_kernel(tc, h_words, h_scales, x, memory, w2_words,
         xm = keep.tile([P, NB, NCT], F32, name="xm")
         ysum = keep.tile([P, NB + 1, 32], F32, name="ysum")
         warm = keep.tile([P, 1], F32, name="warm")
+        idle = keep.tile([P, 512], BF16, name="idle")
         mem_v = mem_t[:].rearrange("p (mb ct i) -> p mb ct i", ct=NCT, i=32)
         base_v = base[:].rearrange("p (mb ct i) -> p mb ct i", ct=NCT, i=32)
 
@@ -86,6 +88,7 @@ def tile_dynamicmemorybank_pb_kernel(tc, h_words, h_scales, x, memory, w2_words,
             load_codes(hcs[(b, mh)], h_words, 0, G, 2 * tok, 2 * tok + 1024)
             load_scales(hs[(2 * b + mh) % 4], h_scales, 0, G, tok, tok + 512)
 
+        nc.gpsimd.memset(idle[:], 0.0)
         nc.gpsimd.memset(warm[:], 0.0)
         nc.scalar.activation(out=warm[:], in_=warm[:], func=ACT.Sigmoid)
         nc.gpsimd.memset(b2row[:], 0.0)
@@ -124,15 +127,15 @@ def tile_dynamicmemorybank_pb_kernel(tc, h_words, h_scales, x, memory, w2_words,
                 )
                 for a in range(4):
                     nc.vector.tensor_copy(out=mfull[:, 32 * a : 32 * a + 32], in_=i4[:])
-        load_h(0, 1)
         xts = {}
         xts[0] = load_x(0)
+        load_h(0, 1)
         xts[1] = load_x(1)
         load_h(1, 0)
         load_h(1, 1)
         lraw = big.tile([P, 32, 256], BF16, name="lraw", tag="big", align_bytes=64)
         for mh in range(NMH):
-            for a in range(4):
+            for a in (0, 2, 1, 3):
                 nc.sync.dma_start(
                     out=lraw[32 * a : 32 * a + 32, 16 * mh : 16 * mh + 16, :],
                     in_=memory[0, 512 * mh : 512 * mh + 512, 256 * a : 256 * a + 256].rearrange(
@@ -205,7 +208,7 @@ def tile_dynamicmemorybank_pb_kernel(tc, h_words, h_scales, x, memory, w2_words,
             size = 512 * n
             rt = fpool.tile([P, 1024], F32, name="rt", align_bytes=64)
             nc.vector.transpose(out=rt[:, 0:size], in_=fin[:, 0:size])
-            for a in range(4):
+            for a in (0, 2, 1, 3):
                 nc.sync.dma_start(
                     out=out[0, 512 * mh : 512 * mh + 512, 256 * a + 32 * c0 : 256 * a + 32 * (c0 + n)].rearrange(
                         "(mb i) c -> i mb c", i=32
@@ -254,6 +257,10 @@ def tile_dynamicmemorybank_pb_kernel(tc, h_words, h_scales, x, memory, w2_words,
         last_use = {}
         for k in range(len(order)):
             last_use[(order[k][0], order[k][1])] = k
+
+        spin = auxp.tile([P, 512], F32, name="aux")
+        for i in range(WARM_MATMULS):
+            nc.tensor.matmul(out=spin[:], lhsT=idle[:, 0:128], rhs=idle[:], start=True, stop=True)
 
         accs = {}
         for k in range(SWEEP):

@@ -104,12 +104,17 @@ def tile_dynamicmemorybank_pb_kernel(tc, h_words, h_scales, x, memory, w2_words,
         later = [[ysum[:], hs[1][:].bitcast(I32)], [hs[2][:].bitcast(I32), hs[3][:].bitcast(I32)], []]
         for run in range(len(HEAD_RUNS)):
             g0, g1 = HEAD_RUNS[run]
-            load_codes(w2raw, w2_words, g0, g1, 0, 2048)
-            load_codes(hcs[(0, 0)], h_words, g0, g1, 0, 1024)
+            if run == 0:
+                load_codes(w2raw, w2_words, 0, 1, 0, 2048)
+                load_codes(hcs[(0, 0)], h_words, 0, 1, 0, 1024)
             load_scales(w2sraw, w2_scales, g0, g1, 0, 1024)
             load_scales(hs[0], h_scales, g0, g1, 0, 512)
             if run == 0:
                 nc.sync.dma_start(out=b2row[0:1, 0, :], in_=b2.rearrange("(o c) -> o c", o=1))
+            else:
+                for g in range(g0, g1):
+                    load_codes(w2raw, w2_words, g, g + 1, 0, 2048)
+                    load_codes(hcs[(0, 0)], h_words, g, g + 1, 0, 1024)
             for g in range(g0, g1):
                 nc.vector.tensor_copy(
                     out=w2c[:, g, :].bitcast(I32).rearrange("p (ct a w) -> p ct a w", ct=8, a=4),
@@ -193,24 +198,26 @@ def tile_dynamicmemorybank_pb_kernel(tc, h_words, h_scales, x, memory, w2_words,
                 out=ysum[:, b + 1, :], in_=zt[:].rearrange("p (cb j) -> p cb j", j=32), axis=AX.X, op=ALU.add
             )
 
-        def mx_pass(acc, b, mh, ct, g):
+        def mx_pass(acc, b, m0, n, ct, g):
+            mh = m0 // 512
+            lo = m0 - 512 * mh
             nc.tensor.matmul_mx(
-                out=acc[:],
+                out=acc[:, 0:n],
                 lhsT=w2c[:, g, 256 * ct : 256 * ct + 256].bitcast(FP4X4),
                 lhsT_scale=w2s[:, g, 128 * ct : 128 * ct + 128],
-                rhs=hcs[(b, mh)][:, g, :].bitcast(FP4X4),
-                rhs_scale=hs[(2 * b + mh) % 4][:, g, :],
+                rhs=hcs[(b, mh)][:, g, 2 * lo : 2 * (lo + n)].bitcast(FP4X4),
+                rhs_scale=hs[(2 * b + mh) % 4][:, g, lo : lo + n],
                 start=(g == 0),
                 stop=(g == G - 1),
             )
 
-        def emit(fin, mh, c0, n):
-            size = 512 * n
+        def emit(fin, m0, nmb, c0, n):
+            size = 32 * nmb * n
             rt = fpool.tile([P, 1024], F32, name="rt", align_bytes=64)
             nc.vector.transpose(out=rt[:, 0:size], in_=fin[:, 0:size])
             for a in (0, 2, 1, 3):
                 nc.sync.dma_start(
-                    out=out[0, 512 * mh : 512 * mh + 512, 256 * a + 32 * c0 : 256 * a + 32 * (c0 + n)].rearrange(
+                    out=out[0, m0 : m0 + 32 * nmb, 256 * a + 32 * c0 : 256 * a + 32 * (c0 + n)].rearrange(
                         "(mb i) c -> i mb c", i=32
                     ),
                     in_=rt[32 * a : 32 * a + 32, 0:size].rearrange("p (mb c) -> p mb c", c=32 * n),
@@ -224,24 +231,24 @@ def tile_dynamicmemorybank_pb_kernel(tc, h_words, h_scales, x, memory, w2_words,
                 out=job["dst"], in0=job["gv"], scalar=-0.25, in1=job["prev"], op0=ALU.mult, op1=ALU.add
             )
             if job["done"]:
-                emit(job["done"][0], job["done"][1], job["done"][2], job["done"][3])
+                emit(job["done"][0], job["done"][1], job["done"][2], job["done"][3], job["done"][4])
 
         def run_jobs():
             while state["next"] < len(waiting) and waiting[state["next"]]["b"] in published:
                 job = waiting[state["next"]]
                 state["next"] += 1
-                b, mh, ct = job["b"], job["mh"], job["ct"]
-                if (b, mh, ct) == (0, 1, 0):
+                b, m0, nmb, ct = job["b"], job["m0"], job["nmb"], job["ct"]
+                if (b, m0, ct) == (0, 512, 0):
                     turn_memory(1)
                 if b == NB - 1:
-                    c0, n = [grp for grp in OUT_GROUPS[mh] if grp[0] <= ct < grp[0] + grp[1]][0]
+                    c0, n = [grp for grp in OUT_GROUPS[m0 // 512] if grp[0] <= ct < grp[0] + grp[1]][0]
                     if ct == c0:
                         state["fin"] = fpool.tile([P, 1024], F32, name="fin", align_bytes=64)
                     fin = state["fin"]
-                    job["dst"] = fin[:, 0 : 512 * n].rearrange("p (mb c i) -> p mb c i", c=n, i=32)[:, :, ct - c0, :]
+                    job["dst"] = fin[:, 0 : 32 * nmb * n].rearrange("p (mb c i) -> p mb c i", c=n, i=32)[:, :, ct - c0, :]
                     if ct == c0 + n - 1:
-                        job["done"] = [fin, mh, c0, n]
-                if (b, mh, ct) == (NB - 1, NMH - 1, NCT - 1):
+                        job["done"] = [fin, m0, nmb, c0, n]
+                if nmb < 16 and state["pending"]:
                     blend(state["pending"])
                     state["pending"] = None
                 nc.vector.scalar_tensor_tensor(
@@ -252,11 +259,13 @@ def tile_dynamicmemorybank_pb_kernel(tc, h_words, h_scales, x, memory, w2_words,
                     blend(state["pending"])
                 state["pending"] = job
 
-        order = [(b, mh, ct) for b in range(2) for mh in range(NMH) for ct in range(NCT)]
-        order.extend([(b, mh, ct) for mh in range(NMH) for ct in range(NCT) for b in (2, 3)])
+        order = [(b, 512 * mh, 512, ct) for b in range(2) for mh in range(NMH) for ct in range(NCT)]
+        order.extend([(b, 512 * mh, 512, ct) for mh in range(NMH) for ct in range(NCT) for b in (2, 3)])
+        order = order[0 : len(order) - 1]
+        order.extend([(NB - 1, 512, 256, NCT - 1), (NB - 1, 768, 256, NCT - 1)])
         last_use = {}
         for k in range(len(order)):
-            last_use[(order[k][0], order[k][1])] = k
+            last_use[(order[k][0], order[k][1] // 512)] = k
 
         spin = auxp.tile([P, 512], F32, name="aux")
         for i in range(WARM_MATMULS):
@@ -267,7 +276,7 @@ def tile_dynamicmemorybank_pb_kernel(tc, h_words, h_scales, x, memory, w2_words,
             accs[k] = accp.tile([P, 512], F32, name="acc")
         for g in range(G):
             for k in range(SWEEP):
-                mx_pass(accs[k], order[k][0], order[k][1], order[k][2], g)
+                mx_pass(accs[k], order[k][0], order[k][1], order[k][2], order[k][3], g)
             if g == 1:
                 sums_on_tensor(b2row, 1, 0)
             if g == 3:
@@ -287,20 +296,21 @@ def tile_dynamicmemorybank_pb_kernel(tc, h_words, h_scales, x, memory, w2_words,
         turn_memory(0)
 
         for k in range(len(order)):
-            b, mh, ct = order[k]
-            rows = slice(16 * mh, 16 * mh + 16)
+            b, m0, n, ct = order[k]
+            mh = m0 // 512
+            rows = slice(m0 // 32, (m0 + n) // 32)
             if k >= SWEEP:
                 accs[k] = accp.tile([P, 512], F32, name="acc")
                 for g in range(G):
-                    mx_pass(accs[k], b, mh, ct, g)
+                    mx_pass(accs[k], b, m0, n, ct, g)
             if b == 0:
                 gv = base_v[:, rows, ct, :]
             else:
                 gt = gpool.tile([P, 512], F32, name="gt")
-                gv = gt[:].rearrange("p (mb i) -> p mb i", i=32)
+                gv = gt[:, 0:n].rearrange("p (mb i) -> p mb i", i=32)
             nc.scalar.activation(
                 out=gv,
-                in_=accs[k][:].rearrange("p (mb i) -> p mb i", i=32),
+                in_=accs[k][:, 0:n].rearrange("p (mb i) -> p mb i", i=32),
                 func=ACT.Sigmoid,
                 bias=b2col[:, ct : ct + 1],
                 scale=1.0,
@@ -312,7 +322,7 @@ def tile_dynamicmemorybank_pb_kernel(tc, h_words, h_scales, x, memory, w2_words,
                     spread(bb + 1, xm[:, bb, :], 1.0 / 1024.0)
                     published.append(bb)
             waiting.append(
-                {"b": b, "mh": mh, "ct": ct, "gv": gv, "mv": mem_v[:, rows, ct, :], "dst": base_v[:, rows, ct, :],
+                {"b": b, "m0": m0, "nmb": n // 32, "ct": ct, "gv": gv, "mv": mem_v[:, rows, ct, :], "dst": base_v[:, rows, ct, :],
                  "prev": mem_v[:, rows, ct, :] if b == 0 else base_v[:, rows, ct, :], "done": None}
             )
             run_jobs()

@@ -27,7 +27,7 @@ SPREAD_AT = {0: 12, 1: 18, 2: 40, 3: 30}
 LATE_TREES = {31: 2}
 TREES = (0, 1)
 VECTOR_SLOTS = (1, 2, 3)
-WARM_MATMULS = 16
+WARM_MATMULS = 8
 
 
 def tile_dynamicmemorybank_pb_kernel(tc, h_words, h_scales, x, memory, w2_words, w2_scales, b2, out):

@@ -22,9 +22,9 @@ NMH = 2
 SWEEP = 7
 HEAD_RUNS = ((0, 1), (1, 4), (4, 8))
 OUT_GROUPS = (((0, 2), (2, 2), (4, 2), (6, 2)), ((0, 2), (2, 2), (4, 2), (6, 1), (7, 1)))
-SUMS_AT = {3: 29}
-SPREAD_AT = {0: 12, 1: 18, 2: 40, 3: 30}
-LATE_TREES = {31: 2}
+SUMS_AT = {3: 34}
+SPREAD_AT = {0: 15, 1: 24, 2: 40, 3: 36}
+LATE_TREES = {27: 2}
 TREES = (0, 1)
 VECTOR_SLOTS = (1, 2, 3)
 WARM_MATMULS = 8

@@ -20,7 +20,7 @@ G = 8
 NCT = 8
 NMH = 2
 SWEEP = 7
-HEAD_RUNS = ((0, 1), (1, 4), (4, 8))
+HEAD_RUNS = ((0, 3), (3, 8))
 OUT_GROUPS = (((0, 2), (2, 2), (4, 2), (6, 2)), ((0, 2), (2, 2), (4, 2), (6, 1), (7, 1)))
 SUMS_AT = {3: 34}
 SPREAD_AT = {0: 15, 1: 24, 2: 40, 3: 36}
@@ -101,7 +101,7 @@ def tile_dynamicmemorybank_pb_kernel(tc, h_words, h_scales, x, memory, w2_words,
         for g0, g1 in HEAD_RUNS:
             nc.vector.memset(w2sraw[:, g0:g1, :].bitcast(I32), 0)
             nc.vector.memset(hs[0][:, g0:g1, :].bitcast(I32), 0)
-        later = [[ysum[:], hs[1][:].bitcast(I32)], [hs[2][:].bitcast(I32), hs[3][:].bitcast(I32)], []]
+        later = [[ysum[:], hs[1][:].bitcast(I32)], [hs[2][:].bitcast(I32), hs[3][:].bitcast(I32)]]
         for run in range(len(HEAD_RUNS)):
             g0, g1 = HEAD_RUNS[run]
             if run == 0:
@@ -109,12 +109,11 @@ def tile_dynamicmemorybank_pb_kernel(tc, h_words, h_scales, x, memory, w2_words,
                 load_codes(hcs[(0, 0)], h_words, 0, 1, 0, 1024)
             load_scales(w2sraw, w2_scales, g0, g1, 0, 1024)
             load_scales(hs[0], h_scales, g0, g1, 0, 512)
+            for g in range(max(g0, 1), g1):
+                load_codes(w2raw, w2_words, g, g + 1, 0, 2048)
+                load_codes(hcs[(0, 0)], h_words, g, g + 1, 0, 1024)
             if run == 0:
                 nc.sync.dma_start(out=b2row[0:1, 0, :], in_=b2.rearrange("(o c) -> o c", o=1))
-            else:
-                for g in range(g0, g1):
-                    load_codes(w2raw, w2_words, g, g + 1, 0, 2048)
-                    load_codes(hcs[(0, 0)], h_words, g, g + 1, 0, 1024)
             for g in range(g0, g1):
                 nc.vector.tensor_copy(
                     out=w2c[:, g, :].bitcast(I32).rearrange("p (ct a w) -> p ct a w", ct=8, a=4),
@@ -277,9 +276,9 @@ def tile_dynamicmemorybank_pb_kernel(tc, h_words, h_scales, x, memory, w2_words,
         for g in range(G):
             for k in range(SWEEP):
                 mx_pass(accs[k], order[k][0], order[k][1], order[k][2], order[k][3], g)
-            if g == 1:
-                sums_on_tensor(b2row, 1, 0)
             if g == 3:
+                sums_on_tensor(b2row, 1, 0)
+            if g == 5:
                 spread(0, b2col[:], 1.0)
 
         for b in TREES:

@@ -21,6 +21,7 @@ NCT = 8
 NMH = 2
 SWEEP = 7
 HEAD_RUNS = ((0, 3), (3, 8))
+CODE_LOADS = (((1, 2), (2, 3)), ((3, 4), (4, 5), (5, 8)))
 OUT_GROUPS = (((0, 2), (2, 2), (4, 2), (6, 2)), ((0, 2), (2, 2), (4, 2), (6, 1), (7, 1)))
 SUMS_AT = {3: 34}
 SPREAD_AT = {0: 15, 1: 24, 2: 40, 3: 36}
@@ -109,9 +110,9 @@ def tile_dynamicmemorybank_pb_kernel(tc, h_words, h_scales, x, memory, w2_words,
                 load_codes(hcs[(0, 0)], h_words, 0, 1, 0, 1024)
             load_scales(w2sraw, w2_scales, g0, g1, 0, 1024)
             load_scales(hs[0], h_scales, g0, g1, 0, 512)
-            for g in range(max(g0, 1), g1):
-                load_codes(w2raw, w2_words, g, g + 1, 0, 2048)
-                load_codes(hcs[(0, 0)], h_words, g, g + 1, 0, 1024)
+            for ga, gb in CODE_LOADS[run]:
+                load_codes(w2raw, w2_words, ga, gb, 0, 2048)
+                load_codes(hcs[(0, 0)], h_words, ga, gb, 0, 1024)
             if run == 0:
                 nc.sync.dma_start(out=b2row[0:1, 0, :], in_=b2.rearrange("(o c) -> o c", o=1))
             for g in range(g0, g1):

from contextlib import ExitStack

import concourse.mybir as mybir
from concourse.masks import make_identity

FLOPS = 2 * 4096 * 4096 * 1024

F32 = mybir.dt.float32
BF16 = mybir.dt.bfloat16
U8 = mybir.dt.uint8
I32 = mybir.dt.int32
FP4X4 = mybir.dt.float4_e2m1fn_x4
ALU = mybir.AluOpType
ACT = mybir.ActivationFunctionType
AX = mybir.AxisListType

P = 128
NB = 4
G = 8
NCT = 8
NMH = 2
SWEEP = 7
HEAD_RUNS = ((0, 3), (3, 8))
CODE_LOADS = (((1, 2), (2, 3)), ((3, 4), (4, 5), (5, 8)))
OUT_GROUPS = (((0, 2), (2, 2), (4, 2), (6, 2)), ((0, 2), (2, 2), (4, 2), (6, 1), (7, 1)))
SUMS_AT = {3: 34}
SPREAD_AT = {0: 15, 1: 24, 2: 40, 3: 36}
LATE_TREES = {27: 2}
TREES = (0, 1)
VECTOR_SLOTS = (1, 2, 3)
WARM_MATMULS = 8


def tile_dynamicmemorybank_pb_kernel(tc, h_words, h_scales, x, memory, w2_words, w2_scales, b2, out):
    nc = tc.nc
    with ExitStack() as ctx:
        ctx.enter_context(tc.manual_schedule(engines={mybir.EngineType.PE, mybir.EngineType.Activation, mybir.EngineType.DVE}))
        keep = ctx.enter_context(tc.tile_pool(name="keep", bufs=1))
        big = ctx.enter_context(tc.tile_pool(name="big", bufs=3))
        hpool = ctx.enter_context(tc.tile_pool(name="hcodes", bufs=4))
        fpool = ctx.enter_context(tc.tile_pool(name="final", bufs=2))
        gpool = ctx.enter_context(tc.tile_pool(name="gate", bufs=11))
        tmp = ctx.enter_context(tc.tile_pool(name="tmp", bufs=2))
        accp = ctx.enter_context(tc.psum_pool(name="acc", bufs=SWEEP))
        auxp = ctx.enter_context(tc.psum_pool(name="aux", bufs=1))

        w2c = keep.tile([P, G, 2048], U8, name="w2c", align_bytes=64)
        w2s = keep.tile([P, G, 1024], U8, name="w2s", align_bytes=64)
        hs = [keep.tile([P, G, 512], U8, name="hs%d" % i, align_bytes=64) for i in range(4)]
        mem_t = keep.tile([P, 8192], BF16, name="mem_t", align_bytes=64)
        base = keep.tile([P, 8192], F32, name="base", align_bytes=64)
        ident = keep.tile([P, P], F32, name="ident")
        i4 = keep.tile([P, 32], F32, name="i4")
        mfull = keep.tile([P, P], F32, name="mfull")
        ones = keep.tile([P, 32], BF16, name="ones")
        b2row = keep.tile([P, 1, 1024], BF16, name="b2row")
        b2col = keep.tile([P, NCT], F32, name="b2col")
        xm = keep.tile([P, NB, NCT], F32, name="xm")
        ysum = keep.tile([P, NB + 1, 32], F32, name="ysum")
        warm = keep.tile([P, 1], F32, name="warm")
        idle = keep.tile([P, 512], BF16, name="idle")
        mem_v = mem_t[:].rearrange("p (mb ct i) -> p mb ct i", ct=NCT, i=32)
        base_v = base[:].rearrange("p (mb ct i) -> p mb ct i", ct=NCT, i=32)

        def load_codes(dst, words, g0, g1, lo, hi):
            nc.sync.dma_start(
                out=dst[:, g0:g1, :].bitcast(I32),
                in_=words[g0:g1, :, lo:hi].rearrange("g p n -> p g n").bitcast(I32),
            )

        def load_scales(dst, scales, g0, g1, lo, hi):
            for q in range(4):
                nc.sync.dma_start(
                    out=dst[32 * q : 32 * q + 4, g0:g1, :].bitcast(I32),
                    in_=scales[g0:g1, 4 * q : 4 * q + 4, lo:hi].rearrange("g r n -> r g n").bitcast(I32),
                )

        def load_x(b):
            xt = big.tile([P, 8, 1024], BF16, name="xt", tag="big", align_bytes=64)
            nc.sync.dma_start(out=xt[:], in_=x[b].rearrange("(p j) c -> p j c", j=8))
            return xt

        hcs = {}
        state = {"pending": None, "fin": None, "next": 0, "aux": None}

        def load_h(b, mh):
            tok = 1024 * b + 512 * mh
            hcs[(b, mh)] = hpool.tile([P, G, 1024], U8, name="hc", align_bytes=64)
            load_codes(hcs[(b, mh)], h_words, 0, G, 2 * tok, 2 * tok + 1024)
            load_scales(hs[(2 * b + mh) % 4], h_scales, 0, G, tok, tok + 512)

        nc.gpsimd.memset(idle[:], 0.0)
        nc.gpsimd.memset(warm[:], 0.0)
        nc.scalar.activation(out=warm[:], in_=warm[:], func=ACT.Sigmoid)
        nc.gpsimd.memset(b2row[:], 0.0)
        nc.gpsimd.memset(ones[:], 1.0)
        make_identity(nc, ident[:])

        w2raw = big.tile([P, G, 2048], U8, name="w2raw", tag="big", align_bytes=64)
        w2sraw = tmp.tile([P, G, 1024], U8, name="w2sraw", tag="s1", align_bytes=64)
        hcs[(0, 0)] = hpool.tile([P, G, 1024], U8, name="hc", align_bytes=64)
        for g0, g1 in HEAD_RUNS:
            nc.vector.memset(w2sraw[:, g0:g1, :].bitcast(I32), 0)
            nc.vector.memset(hs[0][:, g0:g1, :].bitcast(I32), 0)
        later = [[ysum[:], hs[1][:].bitcast(I32)], [hs[2][:].bitcast(I32), hs[3][:].bitcast(I32)]]
        for run in range(len(HEAD_RUNS)):
            g0, g1 = HEAD_RUNS[run]
            if run == 0:
                load_codes(w2raw, w2_words, 0, 1, 0, 2048)
                load_codes(hcs[(0, 0)], h_words, 0, 1, 0, 1024)
            load_scales(w2sraw, w2_scales, g0, g1, 0, 1024)
            load_scales(hs[0], h_scales, g0, g1, 0, 512)
            for ga, gb in CODE_LOADS[run]:
                load_codes(w2raw, w2_words, ga, gb, 0, 2048)
                load_codes(hcs[(0, 0)], h_words, ga, gb, 0, 1024)
            if run == 0:
                nc.sync.dma_start(out=b2row[0:1, 0, :], in_=b2.rearrange("(o c) -> o c", o=1))
            for g in range(g0, g1):
                nc.vector.tensor_copy(
                    out=w2c[:, g, :].bitcast(I32).rearrange("p (ct a w) -> p ct a w", ct=8, a=4),
                    in_=w2raw[:, g, :].bitcast(I32).rearrange("p (a ct w) -> p ct a w", a=4, ct=8),
                )
                nc.vector.tensor_copy(
                    out=w2s[:, g, :].bitcast(I32).rearrange("p (ct a w) -> p ct a w", ct=8, a=4),
                    in_=w2sraw[:, g, :].bitcast(I32).rearrange("p (a ct w) -> p ct a w", a=4, ct=8),
                )
            for view in later[run]:
                nc.vector.memset(view, 0)
            if run == 0:
                nc.vector.tensor_reduce(
                    out=i4[:], in_=ident[:].rearrange("p (q j) -> p j q", q=4), axis=AX.X, op=ALU.add
                )
                for a in range(4):
                    nc.vector.tensor_copy(out=mfull[:, 32 * a : 32 * a + 32], in_=i4[:])
        xts = {}
        xts[0] = load_x(0)
        load_h(0, 1)
        xts[1] = load_x(1)
        load_h(1, 0)
        load_h(1, 1)
        lraw = big.tile([P, 32, 256], BF16, name="lraw", tag="big", align_bytes=64)
        for mh in range(NMH):
            for a in (0, 2, 1, 3):
                nc.sync.dma_start(
                    out=lraw[32 * a : 32 * a + 32, 16 * mh : 16 * mh + 16, :],
                    in_=memory[0, 512 * mh : 512 * mh + 512, 256 * a : 256 * a + 256].rearrange(
                        "(mb i) c -> i mb c", i=32
                    ),
                )

        def sums_on_tensor(src, nj, slot):
            aux = auxp.tile([P, 9, 32], F32, name="aux")
            state["aux"] = aux
            psx = aux[:, 0:8, :]
            for t in range(8):
                for j in range(nj):
                    nc.tensor.matmul(
                        out=psx[:, t, :],
                        lhsT=src[:, j, 128 * t : 128 * t + 128],
                        rhs=ones[:],
                        start=(j == 0),
                        stop=(j == nj - 1),
                    )
            for s in range(4):
                nc.scalar.copy(out=ysum[32 * s : 32 * s + 32, slot, s:32:4], in_=psx[32 * s : 32 * s + 32, :, 0])

        def spread(slot, dst, scale):
            if slot in VECTOR_SLOTS:
                state["aux"] = auxp.tile([P, 9, 32], F32, name="aux")
            ps2 = state["aux"][:, 8, :]
            nc.tensor.matmul(out=ps2, lhsT=mfull[:], rhs=ysum[:, slot, :], start=True, stop=True)
            for a in range(4):
                nc.scalar.activation(
                    out=dst[32 * a : 32 * a + 32, :],
                    in_=ps2[32 * a : 32 * a + 32, 8 * a : 8 * a + 8],
                    func=ACT.Copy,
                    scale=scale,
                )

        def sums_on_vector(b):
            xt = xts[b]
            s1 = []
            for hf in range(2):
                s1.append(tmp.tile([P, 4, 512], F32, name="s1", tag="s1", align_bytes=64))
            zsum = tmp.tile([P, 1024], F32, name="zsum", bufs=1, align_bytes=64)
            zt = tmp.tile([P, 1024], F32, name="zt", bufs=1, align_bytes=64)
            for hf in range(2):
                cs = slice(512 * hf, 512 * hf + 512)
                nc.vector.tensor_tensor(out=s1[hf][:], in0=xt[:, 0:4, cs], in1=xt[:, 4:8, cs], op=ALU.add)
            for hf in range(2):
                nc.vector.tensor_tensor(out=s1[hf][:, 0:2, :], in0=s1[hf][:, 0:2, :], in1=s1[hf][:, 2:4, :], op=ALU.add)
            for hf in range(2):
                nc.vector.tensor_tensor(
                    out=zsum[:, 512 * hf : 512 * hf + 512], in0=s1[hf][:, 0, :], in1=s1[hf][:, 1, :], op=ALU.add
                )
            nc.vector.transpose(out=zt[:], in_=zsum[:])
            nc.vector.tensor_reduce(
                out=ysum[:, b + 1, :], in_=zt[:].rearrange("p (cb j) -> p cb j", j=32), axis=AX.X, op=ALU.add
            )

        def mx_pass(acc, b, m0, n, ct, g):
            mh = m0 // 512
            lo = m0 - 512 * mh
            nc.tensor.matmul_mx(
                out=acc[:, 0:n],
                lhsT=w2c[:, g, 256 * ct : 256 * ct + 256].bitcast(FP4X4),
                lhsT_scale=w2s[:, g, 128 * ct : 128 * ct + 128],
                rhs=hcs[(b, mh)][:, g, 2 * lo : 2 * (lo + n)].bitcast(FP4X4),
                rhs_scale=hs[(2 * b + mh) % 4][:, g, lo : lo + n],
                start=(g == 0),
                stop=(g == G - 1),
            )

        def emit(fin, m0, nmb, c0, n):
            size = 32 * nmb * n
            rt = fpool.tile([P, 1024], F32, name="rt", align_bytes=64)
            nc.vector.transpose(out=rt[:, 0:size], in_=fin[:, 0:size])
            for a in (0, 2, 1, 3):
                nc.sync.dma_start(
                    out=out[0, m0 : m0 + 32 * nmb, 256 * a + 32 * c0 : 256 * a + 32 * (c0 + n)].rearrange(
                        "(mb i) c -> i mb c", i=32
                    ),
                    in_=rt[32 * a : 32 * a + 32, 0:size].rearrange("p (mb c) -> p mb c", c=32 * n),
                )

        waiting = []
        published = []

        def blend(job):
            nc.vector.scalar_tensor_tensor(
                out=job["dst"], in0=job["gv"], scalar=-0.25, in1=job["prev"], op0=ALU.mult, op1=ALU.add
            )
            if job["done"]:
                emit(job["done"][0], job["done"][1], job["done"][2], job["done"][3], job["done"][4])

        def run_jobs():
            while state["next"] < len(waiting) and waiting[state["next"]]["b"] in published:
                job = waiting[state["next"]]
                state["next"] += 1
                b, m0, nmb, ct = job["b"], job["m0"], job["nmb"], job["ct"]
                if (b, m0, ct) == (0, 512, 0):
                    turn_memory(1)
                if b == NB - 1:
                    c0, n = [grp for grp in OUT_GROUPS[m0 // 512] if grp[0] <= ct < grp[0] + grp[1]][0]
                    if ct == c0:
                        state["fin"] = fpool.tile([P, 1024], F32, name="fin", align_bytes=64)
                    fin = state["fin"]
                    job["dst"] = fin[:, 0 : 32 * nmb * n].rearrange("p (mb c i) -> p mb c i", c=n, i=32)[:, :, ct - c0, :]
                    if ct == c0 + n - 1:
                        job["done"] = [fin, m0, nmb, c0, n]
                if nmb < 16 and state["pending"]:
                    blend(state["pending"])
                    state["pending"] = None
                nc.vector.scalar_tensor_tensor(
                    out=job["gv"], in0=job["mv"], scalar=xm[:, b, ct : ct + 1], in1=job["gv"],
                    op0=ALU.subtract, op1=ALU.mult,
                )
                if state["pending"]:
                    blend(state["pending"])
                state["pending"] = job

        order = [(b, 512 * mh, 512, ct) for b in range(2) for mh in range(NMH) for ct in range(NCT)]
        order.extend([(b, 512 * mh, 512, ct) for mh in range(NMH) for ct in range(NCT) for b in (2, 3)])
        order = order[0 : len(order) - 1]
        order.extend([(NB - 1, 512, 256, NCT - 1), (NB - 1, 768, 256, NCT - 1)])
        last_use = {}
        for k in range(len(order)):
            last_use[(order[k][0], order[k][1] // 512)] = k

        spin = auxp.tile([P, 512], F32, name="aux")
        for i in range(WARM_MATMULS):
            nc.tensor.matmul(out=spin[:], lhsT=idle[:, 0:128], rhs=idle[:], start=True, stop=True)

        accs = {}
        for k in range(SWEEP):
            accs[k] = accp.tile([P, 512], F32, name="acc")
        for g in range(G):
            for k in range(SWEEP):
                mx_pass(accs[k], order[k][0], order[k][1], order[k][2], order[k][3], g)
            if g == 3:
                sums_on_tensor(b2row, 1, 0)
            if g == 5:
                spread(0, b2col[:], 1.0)

        for b in TREES:
            sums_on_vector(b)
            xts[b + 2] = load_x(b + 2)
        lflat = lraw[:].rearrange("p mb c -> p (mb c)")

        def turn_memory(mh):
            for q in (2 * mh, 2 * mh + 1):
                nc.vector.transpose(
                    out=mem_t[:, 2048 * q : 2048 * q + 2048], in_=lflat[:, 2048 * q : 2048 * q + 2048]
                )

        turn_memory(0)

        for k in range(len(order)):
            b, m0, n, ct = order[k]
            mh = m0 // 512
            rows = slice(m0 // 32, (m0 + n) // 32)
            if k >= SWEEP:
                accs[k] = accp.tile([P, 512], F32, name="acc")
                for g in range(G):
                    mx_pass(accs[k], b, m0, n, ct, g)
            if b == 0:
                gv = base_v[:, rows, ct, :]
            else:
                gt = gpool.tile([P, 512], F32, name="gt")
                gv = gt[:, 0:n].rearrange("p (mb i) -> p mb i", i=32)
            nc.scalar.activation(
                out=gv,
                in_=accs[k][:, 0:n].rearrange("p (mb i) -> p mb i", i=32),
                func=ACT.Sigmoid,
                bias=b2col[:, ct : ct + 1],
                scale=1.0,
            )
            for bb in range(NB):
                if SUMS_AT.get(bb) == k:
                    sums_on_tensor(xts[bb], 8, bb + 1)
                if SPREAD_AT[bb] == k:
                    spread(bb + 1, xm[:, bb, :], 1.0 / 1024.0)
                    published.append(bb)
            waiting.append(
                {"b": b, "m0": m0, "nmb": n // 32, "ct": ct, "gv": gv, "mv": mem_v[:, rows, ct, :], "dst": base_v[:, rows, ct, :],
                 "prev": mem_v[:, rows, ct, :] if b == 0 else base_v[:, rows, ct, :], "done": None}
            )
            run_jobs()
            if k in LATE_TREES:
                sums_on_vector(LATE_TREES[k])
            if last_use[(b, mh)] == k and b + 2 < NB:
                load_h(b + 2, mh)
        blend(state["pending"])
